import numpy as np
import ml_dtypes


def mxq(x, axis, fmt="e4m3"):
    dtype, down = {"e4m3": (ml_dtypes.float8_e4m3fn, 7), "e5m2": (ml_dtypes.float8_e5m2, 14)}[fmt]
    v = np.moveaxis(np.asarray(x, np.float32).astype(ml_dtypes.bfloat16).astype(np.float64), axis, -1)
    blocks = v.reshape(v.shape[:-1] + (-1, 32))
    amax = np.abs(blocks).max(-1, keepdims=True)
    byte = np.maximum(np.where(amax > 0, np.frexp(amax)[1] - 1 + 127, 0) - down, 1)
    scale = np.exp2(byte - 127.0)
    codes = (blocks / scale).astype(np.float32).astype(dtype).astype(np.float64)
    return np.moveaxis((codes * scale).reshape(v.shape), -1, axis)


WIDE = False


def mx_kscale(k):
    if not WIDE:
        return np.ones(k)
    levels = np.array([30, -30])
    if k % 512:
        return np.exp2(np.random.permutation(np.resize(levels, k // 32))).repeat(32)
    a = np.empty((k // 512, 16))
    for p in range(k // 512):
        a[p, :8] = np.random.permutation(np.resize(levels, 8))
        for g in range(8):
            far = levels[np.abs(levels - a[p, g]) >= 10]
            a[p, g + 8] = far[np.random.randint(len(far))]
    return np.exp2(a.ravel()).repeat(32)


BF16 = ml_dtypes.bfloat16


def bf(x):
    return np.asarray(x, np.float32).astype(BF16)


def f64(x):
    return np.asarray(x).astype(np.float64)


E2M1 = np.array([0.0, 0.5, 1.0, 1.5, 2.0, 3.0, 4.0, 6.0, -0.0, -0.5, -1.0, -1.5, -2.0, -3.0, -4.0, -6.0])


def pack_weight(w, fmt):
    k, n = w.shape
    w = f64(bf(w)).reshape(k // 32, 32, n)
    amax = np.abs(w).max(1)
    if fmt == "e4m3":
        byte = np.frexp(amax)[1] - 1 + 127 - 7
    else:
        mant, ex = np.frexp(amax / 6.0)
        byte = np.where(mant > 0.5, ex, ex - 1) + 127
    byte = np.clip(np.where(amax > 0, byte, 1), 1, 254)
    scaled = (w * np.exp2(127.0 - byte)[:, None, :]).reshape(k, n).astype(np.float32)
    by_word = np.ascontiguousarray(scaled.reshape(k // 512, 128, 4, n).transpose(0, 1, 3, 2))
    if fmt == "e4m3":
        words = by_word.astype(ml_dtypes.float8_e4m3fn).view(np.uint8)
    else:
        c = by_word.astype(ml_dtypes.float4_e2m1fn).view(np.uint8) & 0xF
        words = c[..., 0::2] | (c[..., 1::2] << 4)
    return np.ascontiguousarray(words), np.ascontiguousarray(byte.astype(np.uint8).reshape(k // 512, 16, n))


def unpack_weight(words, scales, fmt):
    g, p, n, _ = words.shape
    if fmt == "e4m3":
        vals = np.ascontiguousarray(words).view(ml_dtypes.float8_e4m3fn).astype(np.float64)
    else:
        nib = np.empty((g, p, n, 4), np.uint8)
        nib[..., 0::2] = words & 0xF
        nib[..., 1::2] = words >> 4
        vals = E2M1[nib]
    vals = vals * np.repeat(np.exp2(scales.astype(np.float64) - 127.0), 8, axis=1)[..., None]
    return vals.transpose(0, 1, 3, 2).reshape(g * 512, n)

def pack4(w):
    words, scales = pack_weight(w, "e2m1")
    return words.reshape(words.shape[0], 128, -1), scales


def unpack4(words, scales):
    return unpack_weight(words.reshape(words.shape[0], 128, -1, 2), scales, "e2m1")


B, T, E, V, H, C = 1, 1024, 1024, 2048, 8, 512
KD = E // H
ROPE_BASE = 10000.0


def rotate_every_two(u):
    u1 = u[..., ::2]
    u2 = u[..., 1::2]
    return np.stack((-u2, u1), axis=-1).reshape(u.shape)


def theta_shift(u, sin, cos):
    return u * cos + rotate_every_two(u) * sin


def setup_inputs():
    s = mx_kscale(E)
    angle = np.arange(T)[:, None] * (1.0 / ROPE_BASE ** (np.repeat(np.arange(KD // 2), 2) * 2.0 / KD))
    x = bf(np.random.standard_normal((B, T, E)) * s)
    sin = bf(np.sin(angle))
    cos = bf(np.cos(angle))
    Wq_words, Wq_scales = pack4(np.random.standard_normal((E, E)) * 0.5 / np.sqrt(E) / s[:, None])
    Wk_words, Wk_scales = pack4(np.random.standard_normal((E, E)) * 2.0 / np.sqrt(E) / s[:, None])
    return {"x": x,
            "sin": sin, "cos": cos,
            "Wq_words": Wq_words, "Wq_scales": Wq_scales,
            "Wk_words": Wk_words, "Wk_scales": Wk_scales}


def reference(x, sin, cos, Wq_words, Wq_scales, Wk_words, Wk_scales):
    xq = mxq(f64(x), 2, "e5m2")
    q = (xq @ unpack4(Wq_words, Wq_scales)).reshape(B, T, H, KD).transpose(0, 2, 1, 3)
    k = ((xq @ unpack4(Wk_words, Wk_scales)) * KD ** -0.5).reshape(B, T, H, KD).transpose(0, 2, 1, 3)
    return theta_shift(q, f64(sin), f64(cos)), theta_shift(k, f64(sin), f64(cos))

@@ -1,0 +1,177 @@
+from contextlib import ExitStack
+
+import concourse.mybir as mybir
+from concourse.masks import make_identity
+
+F32 = mybir.dt.float32
+BF16 = mybir.dt.bfloat16
+U8 = mybir.dt.uint8
+U32 = mybir.dt.uint32
+I32 = mybir.dt.int32
+E5M2X4 = mybir.dt.float8_e5m2_x4
+E2M1X4 = mybir.dt.float4_e2m1fn_x4
+MULT = mybir.AluOpType.mult
+ADD = mybir.AluOpType.add
+
+T = 1024
+E = 1024
+KD = 128
+P = 128
+NT = T // P
+NG = E // 512
+K_SCALE = KD ** -0.5
+FLOPS = 2 * T * E * 2 * E
+V_ADD_PAIRS = 2
+
+
+def tile_multiscaleretention_pa_kernel(tc, x, sin, cos, wq_words, wq_scales, wk_words, wk_scales, out_0, out_1):
+    nc = tc.nc
+    with ExitStack() as ctx:
+        keep = ctx.enter_context(tc.tile_pool(name="keep", bufs=1))
+        grp_pool = ctx.enter_context(tc.tile_pool(name="grp", bufs=3))
+        ab_pool = ctx.enter_context(tc.tile_pool(name="ab", bufs=3))
+        o_pool = ctx.enter_context(tc.tile_pool(name="o", bufs=4))
+        psum_t = ctx.enter_context(tc.psum_pool(name="psum_t", bufs=2))
+        psum_mx = ctx.enter_context(tc.psum_pool(name="psum_mx", bufs=6))
+
+        ident = keep.tile([P, P], F32, name="ident")
+        make_identity(nc, ident[:])
+
+        planes = []
+        for m in range(2):
+            plane = keep.tile([P, NG, E], U8, name="plane%d" % m, align_bytes=64)
+            nc.vector.memset(plane[:].bitcast(I32), 0)
+            planes.append(plane)
+
+        xv = x[0].rearrange("(p i) k -> p i k", i=NT)
+        cosv = cos.rearrange("(p i) c -> p i c", i=NT)
+        sinv = sin.rearrange("(p i) c -> p i c", i=NT)
+        words_in = [wq_words, wk_words]
+        scales_in = [wq_scales, wk_scales]
+        outs = [out_0[0].rearrange("h (p i) c -> p h i c", i=NT), out_1[0].rearrange("h (p i) c -> p h i c", i=NT)]
+
+        xs = []
+        for i in range(NT):
+            xs.append(keep.tile([P, E], BF16, name="x%d" % i))
+        wt = {}
+        for m in range(2):
+            for jj in range(2):
+                wt[(m, jj)] = keep.tile([P, NG, 1024], U8, name="w%d%d" % (m, jj), align_bytes=64)
+        cos_a = keep.tile([P, 2, KD], BF16, name="cos_a")
+        cos_b = keep.tile([P, NT - 2, KD], BF16, name="cos_b")
+        sin_a = keep.tile([P, 2, KD], BF16, name="sin_a")
+        sin_b = keep.tile([P, NT - 2, KD], BF16, name="sin_b")
+
+        def load_x(i):
+            nc.sync.dma_start(out=xs[i][:], in_=xv[:, i, :])
+
+        def load_scales(m):
+            for q in range(4):
+                nc.sync.dma_start(
+                    out=planes[m][32 * q : 32 * q + 4, :, :].bitcast(I32),
+                    in_=scales_in[m][:, 4 * q : 4 * q + 4, :].rearrange("g r n -> r g n").bitcast(I32),
+                )
+
+        def load_words(m, jj):
+            nc.sync.dma_start(
+                out=wt[(m, jj)][:].bitcast(I32),
+                in_=words_in[m].rearrange("g p n -> p g n")[:, :, 1024 * jj : 1024 * (jj + 1)].bitcast(I32),
+            )
+
+        load_x(0)
+        load_scales(0)
+        load_words(0, 0)
+        load_x(1)
+        nc.sync.dma_start(out=cos_a[:], in_=cosv[:, 0:2, :])
+        nc.sync.dma_start(out=sin_a[:], in_=sinv[:, 0:2, :])
+        load_words(0, 1)
+        load_scales(1)
+        load_words(1, 0)
+        load_words(1, 1)
+        load_x(2)
+        load_x(3)
+        nc.sync.dma_start(out=cos_b[:], in_=cosv[:, 2:NT, :])
+        nc.sync.dma_start(out=sin_b[:], in_=sinv[:, 2:NT, :])
+        for i in range(4, NT):
+            load_x(i)
+
+        for s in (sin_a, sin_b):
+            nc.gpsimd.tensor_scalar(out=s[:, :, 0:KD:2], in0=s[:, :, 0:KD:2], scalar1=-1.0, scalar2=0.0, op0=MULT, op1=ADD)
+
+        def cos_of(i):
+            return cos_a[:, i, :] if i < 2 else cos_b[:, i - 2, :]
+
+        def sin_of(i):
+            return sin_a[:, i, :] if i < 2 else sin_b[:, i - 2, :]
+
+        xc = keep.tile([P, NT, NG * P], U32, name="xc", align_bytes=64)
+        xsc = keep.tile([P, NT, NG * P], U8, name="xsc", align_bytes=64)
+
+        def prep(i):
+            words = xs[i][:].bitcast(F32)
+            xt = psum_t.tile([P, NG, 2, P], F32, name="xt")
+            for g in range(NG):
+                for u in range(2):
+                    nc.tensor.transpose(xt[:, g, u, :], words[:, 256 * g + u : 256 * (g + 1) : 2], ident[:])
+            grp = grp_pool.tile([P, NG, P, 4], BF16, name="grp", align_bytes=64)
+            nc.scalar.copy(out=grp[:].bitcast(F32), in_=xt[:].rearrange("p g u r -> p g r u"))
+            nc.vector.quantize_mx(
+                out=xc[:, i, :].bitcast(E5M2X4),
+                scales=xsc[:, i, :],
+                in_=grp[:].rearrange("p g r t -> p (g r t)"),
+            )
+
+        def unit(i, m, jj, a_out, b_out):
+            acc = psum_mx.tile([P, 512], F32, name="acc")
+            for g in range(NG):
+                nc.tensor.matmul_mx(
+                    out=acc[:],
+                    lhsT=xc[:, i, P * g : P * (g + 1)].bitcast(E5M2X4),
+                    lhsT_scale=xsc[:, i, P * g : P * (g + 1)],
+                    rhs=wt[(m, jj)][:, g, :].bitcast(E2M1X4),
+                    rhs_scale=planes[m][:, g, 512 * jj : 512 * (jj + 1)],
+                    start=(g == 0),
+                    stop=(g == NG - 1),
+                )
+            shape4 = [P, 4, KD // 2, 2]
+            u_nat = acc[:].rearrange("p (h n e) -> p h n e", h=4, e=2)
+            u_swp = u_nat[:, :, :, ::-1]
+            cos4 = cos_of(i).rearrange("p (n e) -> p n e", e=2).unsqueeze(1).to_broadcast(shape4)
+            sin4 = sin_of(i).rearrange("p (n e) -> p n e", e=2).unsqueeze(1).to_broadcast(shape4)
+            a4 = a_out.rearrange("p (h n e) -> p h n e", h=4, e=2)
+            b4 = b_out.rearrange("p (h n e) -> p h n e", h=4, e=2)
+            if m == 0:
+                nc.vector.tensor_tensor(out=a4, in0=u_nat, in1=cos4, op=MULT)
+                nc.vector.tensor_tensor(out=b4, in0=u_swp, in1=sin4, op=MULT)
+            else:
+                nc.vector.scalar_tensor_tensor(out=a4, in0=u_nat, scalar=K_SCALE, in1=cos4, op0=MULT, op1=MULT)
+                nc.vector.scalar_tensor_tensor(out=b4, in0=u_swp, scalar=K_SCALE, in1=sin4, op0=MULT, op1=MULT)
+
+        def add_and_store(eng, a, m, jj, a2, b2):
+            o = o_pool.tile([P, 4, 2, KD], F32, name="o")
+            eng.tensor_tensor(
+                out=o[:],
+                in0=a2[:].rearrange("p i (h c) -> p h i c", h=4),
+                in1=b2[:].rearrange("p i (h c) -> p h i c", h=4),
+                op=ADD,
+            )
+            nc.sync.dma_start(out=outs[m][:, 4 * jj : 4 * jj + 4, 2 * a : 2 * a + 2, :], in_=o[:])
+
+        prep(0)
+        prep(1)
+        late = []
+        for a in range(NT // 2):
+            for j in range(4):
+                m, jj = divmod(j, 2)
+                a2 = ab_pool.tile([P, 2, 512], F32, name="a2")
+                b2 = ab_pool.tile([P, 2, 512], F32, name="b2")
+                for ii in range(2):
+                    unit(2 * a + ii, m, jj, a2[:, ii, :], b2[:, ii, :])
+                if a + 1 < NT // 2 and j in (1, 2):
+                    prep(2 * a + 1 + j)
+                if a == NT // 2 - 1 and j >= 4 - V_ADD_PAIRS:
+                    late.append((a, m, jj, a2, b2))
+                else:
+                    add_and_store(nc.gpsimd, a, m, jj, a2, b2)
+        for a, m, jj, a2, b2 in late:
+            add_and_store(nc.vector, a, m, jj, a2, b2)

@@ -21,18 +21,25 @@ NT = T // P
 NG = E // 512
 K_SCALE = KD ** -0.5
 FLOPS = 2 * T * E * 2 * E
-V_ADD_PAIRS = 2
+
+X_GROUPS = [(0, 1), (1, 1), (2, 2), (4, 4)]
+LOOK = 4
+PLAIN = [(0, 0), (0, 1), (1, 0)]
+B_LAG = 9
 
 
 def tile_multiscaleretention_pa_kernel(tc, x, sin, cos, wq_words, wq_scales, wk_words, wk_scales, out_0, out_1):
     nc = tc.nc
     with ExitStack() as ctx:
+        ctx.enter_context(tc.manual_schedule())
         keep = ctx.enter_context(tc.tile_pool(name="keep", bufs=1))
-        grp_pool = ctx.enter_context(tc.tile_pool(name="grp", bufs=3))
-        ab_pool = ctx.enter_context(tc.tile_pool(name="ab", bufs=3))
+        ab_pool = ctx.enter_context(tc.tile_pool(name="ab", bufs=6))
+        cp_pool = ctx.enter_context(tc.tile_pool(name="cp", bufs=4))
+        u_pool = ctx.enter_context(tc.tile_pool(name="u", bufs=2))
         o_pool = ctx.enter_context(tc.tile_pool(name="o", bufs=4))
-        psum_t = ctx.enter_context(tc.psum_pool(name="psum_t", bufs=2))
-        psum_mx = ctx.enter_context(tc.psum_pool(name="psum_mx", bufs=6))
+        oc_pool = ctx.enter_context(tc.tile_pool(name="oc", bufs=6))
+        psum_t = ctx.enter_context(tc.psum_pool(name="psum_t", bufs=3))
+        psum_mx = ctx.enter_context(tc.psum_pool(name="psum_mx", bufs=LOOK + 1))
 
         ident = keep.tile([P, P], F32, name="ident")
         make_identity(nc, ident[:])
@@ -50,9 +57,11 @@ def tile_multiscaleretention_pa_kernel(tc, x, sin, cos, wq_words, wq_scales, wk_
         scales_in = [wq_scales, wk_scales]
         outs = [out_0[0].rearrange("h (p i) c -> p h i c", i=NT), out_1[0].rearrange("h (p i) c -> p h i c", i=NT)]
 
-        xs = []
-        for i in range(NT):
-            xs.append(keep.tile([P, E], BF16, name="x%d" % i))
+        xg = []
+        grps = []
+        for n, (i0, cnt) in enumerate(X_GROUPS):
+            xg.append(keep.tile([P, cnt, E], BF16, name="xg%d" % n))
+            grps.append(keep.tile([P, NG, cnt, P, 4], BF16, name="grp%d" % n, align_bytes=64))
         wt = {}
         for m in range(2):
             for jj in range(2):
@@ -62,8 +71,9 @@ def tile_multiscaleretention_pa_kernel(tc, x, sin, cos, wq_words, wq_scales, wk_
         sin_a = keep.tile([P, 2, KD], BF16, name="sin_a")
         sin_b = keep.tile([P, NT - 2, KD], BF16, name="sin_b")
 
-        def load_x(i):
-            nc.sync.dma_start(out=xs[i][:], in_=xv[:, i, :])
+        def load_x(n):
+            i0, cnt = X_GROUPS[n]
+            nc.sync.dma_start(out=xg[n][:], in_=xv[:, i0 : i0 + cnt, :])
 
         def load_scales(m):
             for q in range(4):
@@ -79,23 +89,21 @@ def tile_multiscaleretention_pa_kernel(tc, x, sin, cos, wq_words, wq_scales, wk_
             )
 
         load_x(0)
-        load_scales(0)
         load_words(0, 0)
+        load_scales(0)
         load_x(1)
-        nc.sync.dma_start(out=cos_a[:], in_=cosv[:, 0:2, :])
         nc.sync.dma_start(out=sin_a[:], in_=sinv[:, 0:2, :])
+        nc.sync.dma_start(out=cos_a[:], in_=cosv[:, 0:2, :])
         load_words(0, 1)
+        load_x(2)
         load_scales(1)
         load_words(1, 0)
-        load_words(1, 1)
-        load_x(2)
-        load_x(3)
-        nc.sync.dma_start(out=cos_b[:], in_=cosv[:, 2:NT, :])
         nc.sync.dma_start(out=sin_b[:], in_=sinv[:, 2:NT, :])
-        for i in range(4, NT):
-            load_x(i)
+        nc.sync.dma_start(out=cos_b[:], in_=cosv[:, 2:NT, :])
+        load_x(3)
+        load_words(1, 1)
 
-        for s in (sin_a, sin_b):
+        def flip(s):
             nc.gpsimd.tensor_scalar(out=s[:, :, 0:KD:2], in0=s[:, :, 0:KD:2], scalar1=-1.0, scalar2=0.0, op0=MULT, op1=ADD)
 
         def cos_of(i):
@@ -104,42 +112,117 @@ def tile_multiscaleretention_pa_kernel(tc, x, sin, cos, wq_words, wq_scales, wk_
         def sin_of(i):
             return sin_a[:, i, :] if i < 2 else sin_b[:, i - 2, :]
 
-        xc = keep.tile([P, NT, NG * P], U32, name="xc", align_bytes=64)
-        xsc = keep.tile([P, NT, NG * P], U8, name="xsc", align_bytes=64)
+        perm = keep.tile([P, P], F32, name="perm")
+        nc.gpsimd.tensor_copy(
+            out=perm[:].rearrange("p (n e) -> p n e", e=2),
+            in_=ident[:].rearrange("p (n e) -> p n e", e=2)[:, :, ::-1],
+        )
+        ident_bf = keep.tile([P, P], BF16, name="ident_bf")
+        nc.gpsimd.tensor_copy(out=ident_bf[:], in_=ident[:])
+        flip(sin_a)
+        flip(sin_b)
 
-        def prep(i):
-            words = xs[i][:].bitcast(F32)
+        xc = keep.tile([P, 2, NG, 4, P], U32, name="xc", align_bytes=64)
+        xsc = keep.tile([P, 2, NG, 4, P], U8, name="xsc", align_bytes=64)
+
+        def turn(n, c):
+            words = xg[n][:, c, :].bitcast(F32)
             xt = psum_t.tile([P, NG, 2, P], F32, name="xt")
             for g in range(NG):
                 for u in range(2):
                     nc.tensor.transpose(xt[:, g, u, :], words[:, 256 * g + u : 256 * (g + 1) : 2], ident[:])
-            grp = grp_pool.tile([P, NG, P, 4], BF16, name="grp", align_bytes=64)
-            nc.scalar.copy(out=grp[:].bitcast(F32), in_=xt[:].rearrange("p g u r -> p g r u"))
-            nc.vector.quantize_mx(
-                out=xc[:, i, :].bitcast(E5M2X4),
-                scales=xsc[:, i, :],
-                in_=grp[:].rearrange("p g r t -> p (g r t)"),
-            )
+            nc.scalar.copy(out=grps[n][:, :, c].bitcast(F32), in_=xt[:].rearrange("p g u r -> p g r u"))
 
-        def unit(i, m, jj, a_out, b_out):
-            acc = psum_mx.tile([P, 512], F32, name="acc")
-            for g in range(NG):
-                nc.tensor.matmul_mx(
-                    out=acc[:],
-                    lhsT=xc[:, i, P * g : P * (g + 1)].bitcast(E5M2X4),
-                    lhsT_scale=xsc[:, i, P * g : P * (g + 1)],
-                    rhs=wt[(m, jj)][:, g, :].bitcast(E2M1X4),
-                    rhs_scale=planes[m][:, g, 512 * jj : 512 * (jj + 1)],
-                    start=(g == 0),
-                    stop=(g == NG - 1),
+        coded = [0]
+
+        def last_tile(unit):
+            return unit[1] if unit[0] == "A" else 4 * unit[2] + 3
+
+        def quantise(n):
+            i0, cnt = X_GROUPS[n]
+            coded[0] = i0 + cnt
+            hf, il = divmod(i0, 4)
+            if cnt == 4:
+                nc.vector.quantize_mx(
+                    out=xc[:, hf].rearrange("p g i w -> p (g i w)").bitcast(E5M2X4),
+                    scales=xsc[:, hf].rearrange("p g i w -> p (g i w)"),
+                    in_=grps[n][:].rearrange("p g c r t -> p (g c r t)"),
                 )
+            else:
+                for g in range(NG):
+                    nc.vector.quantize_mx(
+                        out=xc[:, hf, g, il : il + cnt, :].rearrange("p i w -> p (i w)").bitcast(E5M2X4),
+                        scales=xsc[:, hf, g, il : il + cnt, :].rearrange("p i w -> p (i w)"),
+                        in_=grps[n][:, g].rearrange("p c r t -> p (c r t)"),
+                    )
+
+        cos_t = keep.tile([P, NT, P], BF16, name="cos_t")
+        sin_t = keep.tile([P, NT, P], BF16, name="sin_t")
+        sin_w = keep.tile([P, NT, KD], BF16, name="sin_w")
+
+        def swap_sin():
+            for dst, src in ((sin_w[:, 0:2, :], sin_a), (sin_w[:, 2:NT, :], sin_b)):
+                nc.scalar.copy(
+                    out=dst.rearrange("p i (n e) -> p (i n) e", e=2),
+                    in_=src[:].rearrange("p i (n e) -> p (i n) e", e=2)[:, :, ::-1],
+                )
+
+        def turn_table(dst, src_of):
+            tt = psum_t.tile([P, NT, P], BF16, name="xt")
+            for i in range(NT):
+                nc.tensor.transpose(tt[:, i, :], src_of(i), ident_bf[:])
+            nc.scalar.copy(out=dst[:], in_=tt[:])
+
+        accs = {}
+        pairs = {}
+        prods = {}
+        sums = {}
+
+        def mx(unit):
+            acc = psum_mx.tile([P, 512], F32, name="acc")
+            accs[unit] = acc
+            if unit[0] == "A":
+                kind, i, m, jj = unit
+                hf, il = divmod(i, 4)
+                for g in range(NG):
+                    nc.tensor.matmul_mx(
+                        out=acc[:],
+                        lhsT=xc[:, hf, g, il, :].bitcast(E5M2X4),
+                        lhsT_scale=xsc[:, hf, g, il, :],
+                        rhs=wt[(m, jj)][:, g, :].bitcast(E2M1X4),
+                        rhs_scale=planes[m][:, g, 512 * jj : 512 * (jj + 1)],
+                        start=(g == 0),
+                        stop=(g == NG - 1),
+                    )
+            else:
+                kind, hh, hf = unit
+                for g in range(NG):
+                    nc.tensor.matmul_mx(
+                        out=acc[:],
+                        lhsT=wt[(1, 1)][:, g, 256 * hh : 256 * (hh + 1)].bitcast(E2M1X4),
+                        lhsT_scale=planes[1][:, g, 512 + P * hh : 512 + P * (hh + 1)],
+                        rhs=xc[:, hf, g].rearrange("p i w -> p (i w)").bitcast(E5M2X4),
+                        rhs_scale=xsc[:, hf, g].rearrange("p i w -> p (i w)"),
+                        start=(g == 0),
+                        stop=(g == NG - 1),
+                    )
+
+        def products_plain(unit):
+            kind, i, m, jj = unit
+            acc = accs[unit]
+            a, ii = divmod(i, 2)
+            if (a, m, jj) not in pairs:
+                a2 = ab_pool.tile([P, 2, 512], F32, name="a2")
+                b2 = ab_pool.tile([P, 2, 512], F32, name="b2")
+                pairs[(a, m, jj)] = (a2, b2)
+            a2, b2 = pairs[(a, m, jj)]
             shape4 = [P, 4, KD // 2, 2]
             u_nat = acc[:].rearrange("p (h n e) -> p h n e", h=4, e=2)
             u_swp = u_nat[:, :, :, ::-1]
             cos4 = cos_of(i).rearrange("p (n e) -> p n e", e=2).unsqueeze(1).to_broadcast(shape4)
             sin4 = sin_of(i).rearrange("p (n e) -> p n e", e=2).unsqueeze(1).to_broadcast(shape4)
-            a4 = a_out.rearrange("p (h n e) -> p h n e", h=4, e=2)
-            b4 = b_out.rearrange("p (h n e) -> p h n e", h=4, e=2)
+            a4 = a2[:, ii, :].rearrange("p (h n e) -> p h n e", h=4, e=2)
+            b4 = b2[:, ii, :].rearrange("p (h n e) -> p h n e", h=4, e=2)
             if m == 0:
                 nc.vector.tensor_tensor(out=a4, in0=u_nat, in1=cos4, op=MULT)
                 nc.vector.tensor_tensor(out=b4, in0=u_swp, in1=sin4, op=MULT)
@@ -147,9 +230,12 @@ def tile_multiscaleretention_pa_kernel(tc, x, sin, cos, wq_words, wq_scales, wk_
                 nc.vector.scalar_tensor_tensor(out=a4, in0=u_nat, scalar=K_SCALE, in1=cos4, op0=MULT, op1=MULT)
                 nc.vector.scalar_tensor_tensor(out=b4, in0=u_swp, scalar=K_SCALE, in1=sin4, op0=MULT, op1=MULT)
 
-        def add_and_store(eng, a, m, jj, a2, b2):
+        def add_plain(unit):
+            kind, i, m, jj = unit
+            a = i // 2
+            a2, b2 = pairs[(a, m, jj)]
             o = o_pool.tile([P, 4, 2, KD], F32, name="o")
-            eng.tensor_tensor(
+            nc.gpsimd.tensor_tensor(
                 out=o[:],
                 in0=a2[:].rearrange("p i (h c) -> p h i c", h=4),
                 in1=b2[:].rearrange("p i (h c) -> p h i c", h=4),
@@ -157,21 +243,103 @@ def tile_multiscaleretention_pa_kernel(tc, x, sin, cos, wq_words, wq_scales, wk_
             )
             nc.sync.dma_start(out=outs[m][:, 4 * jj : 4 * jj + 4, 2 * a : 2 * a + 2, :], in_=o[:])
 
-        prep(0)
-        prep(1)
-        late = []
-        for a in range(NT // 2):
-            for j in range(4):
-                m, jj = divmod(j, 2)
-                a2 = ab_pool.tile([P, 2, 512], F32, name="a2")
-                b2 = ab_pool.tile([P, 2, 512], F32, name="b2")
-                for ii in range(2):
-                    unit(2 * a + ii, m, jj, a2[:, ii, :], b2[:, ii, :])
-                if a + 1 < NT // 2 and j in (1, 2):
-                    prep(2 * a + 1 + j)
-                if a == NT // 2 - 1 and j >= 4 - V_ADD_PAIRS:
-                    late.append((a, m, jj, a2, b2))
+        def tables_of(hf):
+            return (cos_t[:, 4 * hf : 4 * hf + 4, :].rearrange("p i r -> p (i r)"), sin_t[:, 4 * hf : 4 * hf + 4, :].rearrange("p i r -> p (i r)"))
+
+        def products_turned(unit):
+            kind, hh, hf = unit
+            acc = accs[unit]
+            if kind == "C":
+                ac = cp_pool.tile([P, 512], F32, name="ac")
+                bc = cp_pool.tile([P, 512], F32, name="bc")
+                prods[unit] = (ac, bc)
+                cos_s, sin_s = tables_of(hf)
+                nc.vector.tensor_tensor(out=ac[:], in0=acc[:], in1=cos_s, op=MULT)
+                nc.vector.tensor_tensor(out=bc[:], in0=acc[:], in1=sin_s, op=MULT)
+            else:
+                u = u_pool.tile([P, 512], F32, name="u")
+                prods[unit] = u
+                nc.scalar.copy(out=u[:], in_=acc[:])
+
+        def products_pool(unit):
+            kind, hh, hf = unit
+            u = prods[unit]
+            ac = cp_pool.tile([P, 512], F32, name="ag")
+            bc = cp_pool.tile([P, 512], F32, name="bg")
+            prods[unit] = (ac, bc)
+            cos_s, sin_s = tables_of(hf)
+            nc.gpsimd.tensor_tensor(out=ac[:], in0=u[:], in1=cos_s, op=MULT)
+            nc.gpsimd.tensor_tensor(out=bc[:], in0=u[:], in1=sin_s, op=MULT)
+
+        def sum_turned(unit):
+            ac, bc = prods[unit]
+            ct = psum_t.tile([P, 4, KD], F32, name="xt")
+            sums[unit] = ct
+            for blk in range(4):
+                cols = slice(P * blk, P * (blk + 1))
+                nc.tensor.matmul(out=ct[:, blk, :], lhsT=ac[:, cols], rhs=ident[:], is_transpose=True, start=True, stop=False)
+                nc.tensor.matmul(out=ct[:, blk, :], lhsT=bc[:, cols], rhs=perm[:], is_transpose=True, start=False, stop=True)
+
+        def store_turned(unit):
+            kind, hh, hf = unit
+            oc = oc_pool.tile([P, 4, KD], F32, name="oc")
+            nc.scalar.mul(out=oc[:], in_=sums[unit][:], mul=K_SCALE)
+            nc.scalar.dma_start(out=outs[1][:, 4 + hh, 4 * hf : 4 * hf + 4, :], in_=oc[:])
+
+        def plain_units(a):
+            return [("A", 2 * a + ii, m, jj) for m, jj in PLAIN for ii in range(2)]
+
+        seq = [("A", 0, 0, 0), ("A", 0, 0, 1), ("A", 1, 0, 0), ("A", 1, 0, 1), ("A", 0, 1, 0), ("A", 1, 1, 0)]
+        seq += plain_units(1)
+        pair_list = [[("A", 2 * a + ii, m, jj) for ii in range(2)] for a in (2, 3) for m, jj in PLAIN]
+        turned_list = [(hh, hf) for hf in range(2) for hh in range(4)]
+        for tok in "bcpcpcppcpcpcc":
+            if tok == "p":
+                seq += pair_list[0]
+                pair_list = pair_list[1:]
+            else:
+                seq.append(({"c": "C", "b": "B"}[tok],) + turned_list[0])
+                turned_list = turned_list[1:]
+
+        extra = {1: [(quantise, 1)], 5: [(quantise, 2)], 13: [(quantise, 3)]}
+        later = {1: [(turn, 2, 0), (turn, 2, 1)],
+                 3: [(turn_table, cos_t, cos_of), (swap_sin,)],
+                 5: [(turn, 3, 0), (turn, 3, 1)],
+                 7: [(turn_table, sin_t, lambda i: sin_w[:, i, :])],
+                 8: [(turn, 3, 2), (turn, 3, 3)]}
+
+        turn(0, 0)
+        quantise(0)
+        mx(seq[0])
+        turn(1, 0)
+        mx(seq[1])
+        n_seq = len(seq)
+        issued = 2
+        seen = []
+        for idx in range(n_seq + B_LAG + 2):
+            for step in extra.get(idx, ()):
+                step[0](*step[1:])
+            while issued < min(n_seq, idx + LOOK + 1) and last_tile(seq[issued]) < coded[0]:
+                mx(seq[issued])
+                issued += 1
+            for step in later.get(idx, ()):
+                step[0](*step[1:])
+            if 1 <= idx <= n_seq and seq[idx - 1][0] == "C":
+                sum_turned(seq[idx - 1])
+            if B_LAG <= idx < n_seq + B_LAG and seq[idx - B_LAG][0] == "B":
+                sum_turned(seq[idx - B_LAG])
+            if idx < n_seq:
+                unit = seq[idx]
+                if unit[0] == "A":
+                    products_plain(unit)
+                    if ("A", unit[1] ^ 1, unit[2], unit[3]) in seen:
+                        add_plain(unit)
+                    seen.append(unit)
                 else:
-                    add_and_store(nc.gpsimd, a, m, jj, a2, b2)
-        for a, m, jj, a2, b2 in late:
-            add_and_store(nc.vector, a, m, jj, a2, b2)
+                    products_turned(unit)
+                    if unit[0] == "B":
+                        products_pool(unit)
+            if 2 <= idx <= n_seq + 1 and seq[idx - 2][0] == "C":
+                store_turned(seq[idx - 2])
+            if B_LAG + 1 <= idx < n_seq + B_LAG + 1 and seq[idx - B_LAG - 1][0] == "B":
+                store_turned(seq[idx - B_LAG - 1])

@@ -293,7 +293,7 @@ def tile_multiscaleretention_pa_kernel(tc, x, sin, cos, wq_words, wq_scales, wk_
         seq += plain_units(1)
         pair_list = [[("A", 2 * a + ii, m, jj) for ii in range(2)] for a in (2, 3) for m, jj in PLAIN]
         turned_list = [(hh, hf) for hf in range(2) for hh in range(4)]
-        for tok in "bcpcpcppcpcpcc":
+        for tok in "bcccppppppcccc":
             if tok == "p":
                 seq += pair_list[0]
                 pair_list = pair_list[1:]

@@ -26,6 +26,8 @@ X_GROUPS = [(0, 1), (1, 1), (2, 2), (4, 4)]
 LOOK = 4
 PLAIN = [(0, 0), (0, 1), (1, 0)]
 B_LAG = 9
+SPIN_HEAD = 4
+SPIN_GAP = 2
 
 
 def tile_multiscaleretention_pa_kernel(tc, x, sin, cos, wq_words, wq_scales, wk_words, wk_scales, out_0, out_1):
@@ -41,6 +43,15 @@ def tile_multiscaleretention_pa_kernel(tc, x, sin, cos, wq_words, wq_scales, wk_
         psum_t = ctx.enter_context(tc.psum_pool(name="psum_t", bufs=3))
         psum_mx = ctx.enter_context(tc.psum_pool(name="psum_mx", bufs=LOOK + 1))
 
+        warm = keep.tile([P, 512], BF16, name="warm")
+        nc.gpsimd.memset(warm[:], 0.0)
+
+        def spin(n):
+            ps = psum_t.tile([P, 512], F32, name="xt")
+            for k in range(n):
+                nc.tensor.matmul(out=ps[:], lhsT=warm[:, 0:P], rhs=warm[:], start=True, stop=True)
+
+        spin(SPIN_HEAD)
         ident = keep.tile([P, P], F32, name="ident")
         make_identity(nc, ident[:])
 
@@ -309,6 +320,7 @@ def tile_multiscaleretention_pa_kernel(tc, x, sin, cos, wq_words, wq_scales, wk_
                  8: [(turn, 3, 2), (turn, 3, 3)]}
 
         turn(0, 0)
+        spin(SPIN_GAP)
         quantise(0)
         mx(seq[0])
         turn(1, 0)

@@ -210,8 +210,8 @@ def tile_multiscaleretention_pa_kernel(tc, x, sin, cos, wq_words, wq_scales, wk_
                 for g in range(NG):
                     nc.tensor.matmul_mx(
                         out=acc[:],
-                        lhsT=wt[(1, 1)][:, g, 256 * hh : 256 * (hh + 1)].bitcast(E2M1X4),
-                        lhsT_scale=planes[1][:, g, 512 + P * hh : 512 + P * (hh + 1)],
+                        lhsT=wt[(1, hh // 4)][:, g, 256 * (hh % 4) : 256 * (hh % 4 + 1)].bitcast(E2M1X4),
+                        lhsT_scale=planes[1][:, g, P * hh : P * (hh + 1)],
                         rhs=xc[:, hf, g].rearrange("p i w -> p (i w)").bitcast(E5M2X4),
                         rhs_scale=xsc[:, hf, g].rearrange("p i w -> p (i w)"),
                         start=(g == 0),
@@ -295,16 +295,16 @@ def tile_multiscaleretention_pa_kernel(tc, x, sin, cos, wq_words, wq_scales, wk_
             kind, hh, hf = unit
             oc = oc_pool.tile([P, 4, KD], F32, name="oc")
             nc.scalar.mul(out=oc[:], in_=sums[unit][:], mul=K_SCALE)
-            nc.scalar.dma_start(out=outs[1][:, 4 + hh, 4 * hf : 4 * hf + 4, :], in_=oc[:])
+            nc.scalar.dma_start(out=outs[1][:, hh, 4 * hf : 4 * hf + 4, :], in_=oc[:])
 
         def plain_units(a):
             return [("A", 2 * a + ii, m, jj) for m, jj in PLAIN for ii in range(2)]
 
         seq = [("A", 0, 0, 0), ("A", 0, 0, 1), ("A", 1, 0, 0), ("A", 1, 0, 1), ("A", 0, 1, 0), ("A", 1, 1, 0)]
         seq += plain_units(1)
-        pair_list = [[("A", 2 * a + ii, m, jj) for ii in range(2)] for a in (2, 3) for m, jj in PLAIN]
-        turned_list = [(hh, hf) for hf in range(2) for hh in range(4)]
-        for tok in "bcccppppppcccc":
+        pair_list = [[("A", 2 * a + ii, m, jj) for ii in range(2)] for a in (2, 3) for m, jj in PLAIN[:2]]
+        turned_list = [(hh, 0) for hh in range(4, 8)] + [(hh, 1) for hh in range(8)]
+        for tok in "bcccbppcccppcccc":
             if tok == "p":
                 seq += pair_list[0]
                 pair_list = pair_list[1:]

@@ -99,12 +99,13 @@ def tile_multiscaleretention_pa_kernel(tc, x, sin, cos, wq_words, wq_scales, wk_
                 in_=words_in[m].rearrange("g p n -> p g n")[:, :, 1024 * jj : 1024 * (jj + 1)].bitcast(I32),
             )
 
-        load_x(0)
+        for g in range(NG):
+            nc.sync.dma_start(out=xg[0][:, 0, 512 * g : 512 * (g + 1)], in_=xv[:, 0, 512 * g : 512 * (g + 1)])
         load_words(0, 0)
         load_scales(0)
-        load_x(1)
         nc.sync.dma_start(out=sin_a[:], in_=sinv[:, 0:2, :])
         nc.sync.dma_start(out=cos_a[:], in_=cosv[:, 0:2, :])
+        load_x(1)
         load_words(0, 1)
         load_x(2)
         load_scales(1)
@@ -143,6 +144,13 @@ def tile_multiscaleretention_pa_kernel(tc, x, sin, cos, wq_words, wq_scales, wk_
                 for u in range(2):
                     nc.tensor.transpose(xt[:, g, u, :], words[:, 256 * g + u : 256 * (g + 1) : 2], ident[:])
             nc.scalar.copy(out=grps[n][:, :, c].bitcast(F32), in_=xt[:].rearrange("p g u r -> p g r u"))
+
+        def turn_pass(g):
+            words = xg[0][:, 0, :].bitcast(F32)
+            xt = psum_t.tile([P, 2, P], F32, name="xt")
+            for u in range(2):
+                nc.tensor.transpose(xt[:, u, :], words[:, 256 * g + u : 256 * (g + 1) : 2], ident[:])
+            nc.scalar.copy(out=grps[0][:, g, 0].bitcast(F32), in_=xt[:].rearrange("p u r -> p r u"))
 
         coded = [0]
 
@@ -319,7 +327,8 @@ def tile_multiscaleretention_pa_kernel(tc, x, sin, cos, wq_words, wq_scales, wk_
                  7: [(turn_table, sin_t, lambda i: sin_w[:, i, :])],
                  8: [(turn, 3, 2), (turn, 3, 3)]}
 
-        turn(0, 0)
+        turn_pass(0)
+        turn_pass(1)
         spin(SPIN_GAP)
         quantise(0)
         mx(seq[0])

@@ -231,8 +231,8 @@ def tile_multiscaleretention_pa_kernel(tc, x, sin, cos, wq_words, wq_scales, wk_
             acc = accs[unit]
             a, ii = divmod(i, 2)
             if (a, m, jj) not in pairs:
-                a2 = ab_pool.tile([P, 2, 512], F32, name="a2")
-                b2 = ab_pool.tile([P, 2, 512], F32, name="b2")
+                a2 = ab_pool.tile([P, 4, 2, KD], F32, name="a2")
+                b2 = ab_pool.tile([P, 4, 2, KD], F32, name="b2")
                 pairs[(a, m, jj)] = (a2, b2)
             a2, b2 = pairs[(a, m, jj)]
             shape4 = [P, 4, KD // 2, 2]
@@ -240,8 +240,8 @@ def tile_multiscaleretention_pa_kernel(tc, x, sin, cos, wq_words, wq_scales, wk_
             u_swp = u_nat[:, :, :, ::-1]
             cos4 = cos_of(i).rearrange("p (n e) -> p n e", e=2).unsqueeze(1).to_broadcast(shape4)
             sin4 = sin_of(i).rearrange("p (n e) -> p n e", e=2).unsqueeze(1).to_broadcast(shape4)
-            a4 = a2[:, ii, :].rearrange("p (h n e) -> p h n e", h=4, e=2)
-            b4 = b2[:, ii, :].rearrange("p (h n e) -> p h n e", h=4, e=2)
+            a4 = a2[:, :, ii, :].rearrange("p h (n e) -> p h n e", e=2)
+            b4 = b2[:, :, ii, :].rearrange("p h (n e) -> p h n e", e=2)
             if m == 0:
                 nc.vector.tensor_tensor(out=a4, in0=u_nat, in1=cos4, op=MULT)
                 nc.vector.tensor_tensor(out=b4, in0=u_swp, in1=sin4, op=MULT)
@@ -256,8 +256,8 @@ def tile_multiscaleretention_pa_kernel(tc, x, sin, cos, wq_words, wq_scales, wk_
             o = o_pool.tile([P, 4, 2, KD], F32, name="o")
             nc.gpsimd.tensor_tensor(
                 out=o[:],
-                in0=a2[:].rearrange("p i (h c) -> p h i c", h=4),
-                in1=b2[:].rearrange("p i (h c) -> p h i c", h=4),
+                in0=a2[:],
+                in1=b2[:],
                 op=ADD,
             )
             nc.sync.dma_start(out=outs[m][:, 4 * jj : 4 * jj + 4, 2 * a : 2 * a + 2, :], in_=o[:])

@@ -26,8 +26,8 @@ X_GROUPS = [(0, 1), (1, 1), (2, 2), (4, 4)]
 LOOK = 4
 PLAIN = [(0, 0), (0, 1), (1, 0)]
 B_LAG = 9
-SPIN_HEAD = 4
-SPIN_GAP = 2
+SPIN_HEAD = 2
+SPIN_GAP = 1
 
 
 def tile_multiscaleretention_pa_kernel(tc, x, sin, cos, wq_words, wq_scales, wk_words, wk_scales, out_0, out_1):
@@ -43,8 +43,14 @@ def tile_multiscaleretention_pa_kernel(tc, x, sin, cos, wq_words, wq_scales, wk_
         psum_t = ctx.enter_context(tc.psum_pool(name="psum_t", bufs=3))
         psum_mx = ctx.enter_context(tc.psum_pool(name="psum_mx", bufs=LOOK + 1))
 
+        planes = []
+        for m in range(2):
+            planes.append(keep.tile([P, NG, E], U8, name="plane%d" % m, align_bytes=64))
+        nc.gpsimd.memset(planes[0][:].bitcast(F32), 0.0)
+
         warm = keep.tile([P, 512], BF16, name="warm")
-        nc.gpsimd.memset(warm[:], 0.0)
+        nc.vector.memset(warm[:], 0.0)
+        nc.vector.memset(planes[1][:].bitcast(I32), 0)
 
         def spin(n):
             ps = psum_t.tile([P, 512], F32, name="xt")
@@ -54,12 +60,6 @@ def tile_multiscaleretention_pa_kernel(tc, x, sin, cos, wq_words, wq_scales, wk_
         spin(SPIN_HEAD)
         ident = keep.tile([P, P], F32, name="ident")
         make_identity(nc, ident[:])
-
-        planes = []
-        for m in range(2):
-            plane = keep.tile([P, NG, E], U8, name="plane%d" % m, align_bytes=64)
-            nc.vector.memset(plane[:].bitcast(I32), 0)
-            planes.append(plane)
 
         xv = x[0].rearrange("(p i) k -> p i k", i=NT)
         cosv = cos.rearrange("(p i) c -> p i c", i=NT)
@@ -101,11 +101,11 @@ def tile_multiscaleretention_pa_kernel(tc, x, sin, cos, wq_words, wq_scales, wk_
 
         for g in range(NG):
             nc.sync.dma_start(out=xg[0][:, 0, 512 * g : 512 * (g + 1)], in_=xv[:, 0, 512 * g : 512 * (g + 1)])
-        load_words(0, 0)
         load_scales(0)
-        nc.sync.dma_start(out=sin_a[:], in_=sinv[:, 0:2, :])
-        nc.sync.dma_start(out=cos_a[:], in_=cosv[:, 0:2, :])
+        load_words(0, 0)
         load_x(1)
+        nc.sync.dma_start(out=cos_a[:], in_=cosv[:, 0:2, :])
+        nc.sync.dma_start(out=sin_a[:], in_=sinv[:, 0:2, :])
         load_words(0, 1)
         load_x(2)
         load_scales(1)

@@ -25,9 +25,13 @@ FLOPS = 2 * T * E * 2 * E
 X_GROUPS = [(0, 1), (1, 1), (2, 2), (4, 4)]
 LOOK = 4
 PLAIN = [(0, 0), (0, 1), (1, 0)]
-B_LAG = 9
+B_LAG = 7
 SPIN_HEAD = 2
 SPIN_GAP = 1
+Q3_AT = 12
+STORE_LAG = 3
+ADD_MODE = {0: "g", 1: "g", 2: "g", 3: "g", 30: "v", 31: "v"}
+ORDER = "bccpbccpbccpcccp"
 
 
 def tile_multiscaleretention_pa_kernel(tc, x, sin, cos, wq_words, wq_scales, wk_words, wk_scales, out_0, out_1):
@@ -37,9 +41,11 @@ def tile_multiscaleretention_pa_kernel(tc, x, sin, cos, wq_words, wq_scales, wk_
         keep = ctx.enter_context(tc.tile_pool(name="keep", bufs=1))
         ab_pool = ctx.enter_context(tc.tile_pool(name="ab", bufs=6))
         cp_pool = ctx.enter_context(tc.tile_pool(name="cp", bufs=4))
-        u_pool = ctx.enter_context(tc.tile_pool(name="u", bufs=2))
+        u_pool = ctx.enter_context(tc.tile_pool(name="u", bufs=3))
         o_pool = ctx.enter_context(tc.tile_pool(name="o", bufs=4))
         oc_pool = ctx.enter_context(tc.tile_pool(name="oc", bufs=6))
+        o1_pool = ctx.enter_context(tc.tile_pool(name="o1", bufs=6))
+        ab1_pool = ctx.enter_context(tc.tile_pool(name="ab1", bufs=4))
         psum_t = ctx.enter_context(tc.psum_pool(name="psum_t", bufs=3))
         psum_mx = ctx.enter_context(tc.psum_pool(name="psum_mx", bufs=LOOK + 1))
 
@@ -132,7 +138,6 @@ def tile_multiscaleretention_pa_kernel(tc, x, sin, cos, wq_words, wq_scales, wk_
         ident_bf = keep.tile([P, P], BF16, name="ident_bf")
         nc.gpsimd.tensor_copy(out=ident_bf[:], in_=ident[:])
         flip(sin_a)
-        flip(sin_b)
 
         xc = keep.tile([P, 2, NG, 4, P], U32, name="xc", align_bytes=64)
         xsc = keep.tile([P, 2, NG, 4, P], U8, name="xsc", align_bytes=64)
@@ -180,6 +185,7 @@ def tile_multiscaleretention_pa_kernel(tc, x, sin, cos, wq_words, wq_scales, wk_
         sin_w = keep.tile([P, NT, KD], BF16, name="sin_w")
 
         def swap_sin():
+            nc.scalar.mul(out=sin_b[:, :, 0:KD:2], in_=sin_b[:, :, 0:KD:2], mul=-1.0)
             for dst, src in ((sin_w[:, 0:2, :], sin_a), (sin_w[:, 2:NT, :], sin_b)):
                 nc.scalar.copy(
                     out=dst.rearrange("p i (n e) -> p (i n) e", e=2),
@@ -194,6 +200,9 @@ def tile_multiscaleretention_pa_kernel(tc, x, sin, cos, wq_words, wq_scales, wk_
 
         accs = {}
         pairs = {}
+        stores = []
+        step = [0]
+        singles = {}
         prods = {}
         sums = {}
 
@@ -226,15 +235,21 @@ def tile_multiscaleretention_pa_kernel(tc, x, sin, cos, wq_words, wq_scales, wk_
                         stop=(g == NG - 1),
                     )
 
-        def products_plain(unit):
+        def products_plain(unit, alone):
             kind, i, m, jj = unit
             acc = accs[unit]
             a, ii = divmod(i, 2)
-            if (a, m, jj) not in pairs:
-                a2 = ab_pool.tile([P, 4, 2, KD], F32, name="a2")
-                b2 = ab_pool.tile([P, 4, 2, KD], F32, name="b2")
-                pairs[(a, m, jj)] = (a2, b2)
-            a2, b2 = pairs[(a, m, jj)]
+            if alone:
+                a1 = ab1_pool.tile([P, 4, 1, KD], F32, name="a1")
+                b1 = ab1_pool.tile([P, 4, 1, KD], F32, name="b1")
+                singles[unit] = (a1, b1)
+                a2, b2, ii = a1, b1, 0
+            else:
+                if (a, m, jj) not in pairs:
+                    a2 = ab_pool.tile([P, 4, 2, KD], F32, name="a2")
+                    b2 = ab_pool.tile([P, 4, 2, KD], F32, name="b2")
+                    pairs[(a, m, jj)] = (a2, b2)
+                a2, b2 = pairs[(a, m, jj)]
             shape4 = [P, 4, KD // 2, 2]
             u_nat = acc[:].rearrange("p (h n e) -> p h n e", h=4, e=2)
             u_swp = u_nat[:, :, :, ::-1]
@@ -260,7 +275,14 @@ def tile_multiscaleretention_pa_kernel(tc, x, sin, cos, wq_words, wq_scales, wk_
                 in1=b2[:],
                 op=ADD,
             )
-            nc.sync.dma_start(out=outs[m][:, 4 * jj : 4 * jj + 4, 2 * a : 2 * a + 2, :], in_=o[:])
+            stores.append((step[0] + STORE_LAG, outs[m][:, 4 * jj : 4 * jj + 4, 2 * a : 2 * a + 2, :], o))
+
+        def add_single(unit, engine):
+            kind, i, m, jj = unit
+            a1, b1 = singles[unit]
+            o = o1_pool.tile([P, 4, KD], F32, name="o1")
+            engine.tensor_tensor(out=o[:], in0=a1[:, :, 0, :], in1=b1[:, :, 0, :], op=ADD)
+            stores.append((step[0] + (STORE_LAG if engine is nc.gpsimd else 0), outs[m][:, 4 * jj : 4 * jj + 4, i, :], o))
 
         def tables_of(hf):
             return (cos_t[:, 4 * hf : 4 * hf + 4, :].rearrange("p i r -> p (i r)"), sin_t[:, 4 * hf : 4 * hf + 4, :].rearrange("p i r -> p (i r)"))
@@ -303,7 +325,7 @@ def tile_multiscaleretention_pa_kernel(tc, x, sin, cos, wq_words, wq_scales, wk_
             kind, hh, hf = unit
             oc = oc_pool.tile([P, 4, KD], F32, name="oc")
             nc.scalar.mul(out=oc[:], in_=sums[unit][:], mul=K_SCALE)
-            nc.scalar.dma_start(out=outs[1][:, hh, 4 * hf : 4 * hf + 4, :], in_=oc[:])
+            nc.sync.dma_start(out=outs[1][:, hh, 4 * hf : 4 * hf + 4, :], in_=oc[:])
 
         def plain_units(a):
             return [("A", 2 * a + ii, m, jj) for m, jj in PLAIN for ii in range(2)]
@@ -312,7 +334,7 @@ def tile_multiscaleretention_pa_kernel(tc, x, sin, cos, wq_words, wq_scales, wk_
         seq += plain_units(1)
         pair_list = [[("A", 2 * a + ii, m, jj) for ii in range(2)] for a in (2, 3) for m, jj in PLAIN[:2]]
         turned_list = [(hh, 0) for hh in range(4, 8)] + [(hh, 1) for hh in range(8)]
-        for tok in "bcccbppcccppcccc":
+        for tok in ORDER:
             if tok == "p":
                 seq += pair_list[0]
                 pair_list = pair_list[1:]
@@ -320,12 +342,12 @@ def tile_multiscaleretention_pa_kernel(tc, x, sin, cos, wq_words, wq_scales, wk_
                 seq.append(({"c": "C", "b": "B"}[tok],) + turned_list[0])
                 turned_list = turned_list[1:]
 
-        extra = {1: [(quantise, 1)], 5: [(quantise, 2)], 13: [(quantise, 3)]}
+        extra = {1: [(quantise, 1)], 5: [(quantise, 2)], Q3_AT: [(quantise, 3)]}
         later = {1: [(turn, 2, 0), (turn, 2, 1)],
                  3: [(turn_table, cos_t, cos_of), (swap_sin,)],
                  5: [(turn, 3, 0), (turn, 3, 1)],
-                 7: [(turn_table, sin_t, lambda i: sin_w[:, i, :])],
-                 8: [(turn, 3, 2), (turn, 3, 3)]}
+                 6: [(turn, 3, 2), (turn, 3, 3)],
+                 8: [(turn_table, sin_t, lambda i: sin_w[:, i, :])]}
 
         turn_pass(0)
         turn_pass(1)
@@ -338,13 +360,14 @@ def tile_multiscaleretention_pa_kernel(tc, x, sin, cos, wq_words, wq_scales, wk_
         issued = 2
         seen = []
         for idx in range(n_seq + B_LAG + 2):
-            for step in extra.get(idx, ()):
-                step[0](*step[1:])
+            step[0] = idx
+            for job in extra.get(idx, ()):
+                job[0](*job[1:])
             while issued < min(n_seq, idx + LOOK + 1) and last_tile(seq[issued]) < coded[0]:
                 mx(seq[issued])
                 issued += 1
-            for step in later.get(idx, ()):
-                step[0](*step[1:])
+            for job in later.get(idx, ()):
+                job[0](*job[1:])
             if 1 <= idx <= n_seq and seq[idx - 1][0] == "C":
                 sum_turned(seq[idx - 1])
             if B_LAG <= idx < n_seq + B_LAG and seq[idx - B_LAG][0] == "B":
@@ -352,14 +375,23 @@ def tile_multiscaleretention_pa_kernel(tc, x, sin, cos, wq_words, wq_scales, wk_
             if idx < n_seq:
                 unit = seq[idx]
                 if unit[0] == "A":
-                    products_plain(unit)
-                    if ("A", unit[1] ^ 1, unit[2], unit[3]) in seen:
+                    mode = ADD_MODE.get(idx, "p")
+                    products_plain(unit, mode != "p")
+                    if mode == "g":
+                        add_single(unit, nc.gpsimd)
+                    elif mode == "v":
+                        add_single(unit, nc.vector)
+                    elif ("A", unit[1] ^ 1, unit[2], unit[3]) in seen:
                         add_plain(unit)
                     seen.append(unit)
                 else:
                     products_turned(unit)
                     if unit[0] == "B":
                         products_pool(unit)
+            for due, view, tile_ in list(stores):
+                if due <= idx:
+                    nc.sync.dma_start(out=view, in_=tile_[:])
+                    stores.remove((due, view, tile_))
             if 2 <= idx <= n_seq + 1 and seq[idx - 2][0] == "C":
                 store_turned(seq[idx - 2])
             if B_LAG + 1 <= idx < n_seq + B_LAG + 1 and seq[idx - B_LAG - 1][0] == "B":

from contextlib import ExitStack

import concourse.mybir as mybir
from concourse.masks import make_identity

F32 = mybir.dt.float32
BF16 = mybir.dt.bfloat16
U8 = mybir.dt.uint8
U32 = mybir.dt.uint32
I32 = mybir.dt.int32
E5M2X4 = mybir.dt.float8_e5m2_x4
E2M1X4 = mybir.dt.float4_e2m1fn_x4
MULT = mybir.AluOpType.mult
ADD = mybir.AluOpType.add

T = 1024
E = 1024
KD = 128
P = 128
NT = T // P
NG = E // 512
K_SCALE = KD ** -0.5
FLOPS = 2 * T * E * 2 * E

X_GROUPS = [(0, 1), (1, 1), (2, 2), (4, 4)]
LOOK = 4
PLAIN = [(0, 0), (0, 1), (1, 0)]
B_LAG = 7
SPIN_HEAD = 2
SPIN_GAP = 1
Q3_AT = 12
STORE_LAG = 3
ADD_MODE = {0: "g", 1: "g", 2: "g", 3: "g", 30: "v", 31: "v"}
ORDER = "bccpbccpbccpcccp"


def tile_multiscaleretention_pa_kernel(tc, x, sin, cos, wq_words, wq_scales, wk_words, wk_scales, out_0, out_1):
    nc = tc.nc
    with ExitStack() as ctx:
        ctx.enter_context(tc.manual_schedule())
        keep = ctx.enter_context(tc.tile_pool(name="keep", bufs=1))
        ab_pool = ctx.enter_context(tc.tile_pool(name="ab", bufs=6))
        cp_pool = ctx.enter_context(tc.tile_pool(name="cp", bufs=4))
        u_pool = ctx.enter_context(tc.tile_pool(name="u", bufs=3))
        o_pool = ctx.enter_context(tc.tile_pool(name="o", bufs=4))
        oc_pool = ctx.enter_context(tc.tile_pool(name="oc", bufs=6))
        o1_pool = ctx.enter_context(tc.tile_pool(name="o1", bufs=6))
        ab1_pool = ctx.enter_context(tc.tile_pool(name="ab1", bufs=4))
        psum_t = ctx.enter_context(tc.psum_pool(name="psum_t", bufs=3))
        psum_mx = ctx.enter_context(tc.psum_pool(name="psum_mx", bufs=LOOK + 1))

        planes = []
        for m in range(2):
            planes.append(keep.tile([P, NG, E], U8, name="plane%d" % m, align_bytes=64))
        nc.gpsimd.memset(planes[0][:].bitcast(F32), 0.0)

        warm = keep.tile([P, 512], BF16, name="warm")
        nc.vector.memset(warm[:], 0.0)
        nc.vector.memset(planes[1][:].bitcast(I32), 0)

        def spin(n):
            ps = psum_t.tile([P, 512], F32, name="xt")
            for k in range(n):
                nc.tensor.matmul(out=ps[:], lhsT=warm[:, 0:P], rhs=warm[:], start=True, stop=True)

        spin(SPIN_HEAD)
        ident = keep.tile([P, P], F32, name="ident")
        make_identity(nc, ident[:])

        xv = x[0].rearrange("(p i) k -> p i k", i=NT)
        cosv = cos.rearrange("(p i) c -> p i c", i=NT)
        sinv = sin.rearrange("(p i) c -> p i c", i=NT)
        words_in = [wq_words, wk_words]
        scales_in = [wq_scales, wk_scales]
        outs = [out_0[0].rearrange("h (p i) c -> p h i c", i=NT), out_1[0].rearrange("h (p i) c -> p h i c", i=NT)]

        xg = []
        grps = []
        for n, (i0, cnt) in enumerate(X_GROUPS):
            xg.append(keep.tile([P, cnt, E], BF16, name="xg%d" % n))
            grps.append(keep.tile([P, NG, cnt, P, 4], BF16, name="grp%d" % n, align_bytes=64))
        wt = {}
        for m in range(2):
            for jj in range(2):
                wt[(m, jj)] = keep.tile([P, NG, 1024], U8, name="w%d%d" % (m, jj), align_bytes=64)
        cos_a = keep.tile([P, 2, KD], BF16, name="cos_a")
        cos_b = keep.tile([P, NT - 2, KD], BF16, name="cos_b")
        sin_a = keep.tile([P, 2, KD], BF16, name="sin_a")
        sin_b = keep.tile([P, NT - 2, KD], BF16, name="sin_b")

        def load_x(n):
            i0, cnt = X_GROUPS[n]
            nc.sync.dma_start(out=xg[n][:], in_=xv[:, i0 : i0 + cnt, :])

        def load_scales(m):
            for q in range(4):
                nc.sync.dma_start(
                    out=planes[m][32 * q : 32 * q + 4, :, :].bitcast(I32),
                    in_=scales_in[m][:, 4 * q : 4 * q + 4, :].rearrange("g r n -> r g n").bitcast(I32),
                )

        def load_words(m, jj):
            nc.sync.dma_start(
                out=wt[(m, jj)][:].bitcast(I32),
                in_=words_in[m].rearrange("g p n -> p g n")[:, :, 1024 * jj : 1024 * (jj + 1)].bitcast(I32),
            )

        for g in range(NG):
            nc.sync.dma_start(out=xg[0][:, 0, 512 * g : 512 * (g + 1)], in_=xv[:, 0, 512 * g : 512 * (g + 1)])
        load_scales(0)
        load_words(0, 0)
        load_x(1)
        nc.sync.dma_start(out=cos_a[:], in_=cosv[:, 0:2, :])
        nc.sync.dma_start(out=sin_a[:], in_=sinv[:, 0:2, :])
        load_words(0, 1)
        load_x(2)
        load_scales(1)
        load_words(1, 0)
        nc.sync.dma_start(out=sin_b[:], in_=sinv[:, 2:NT, :])
        nc.sync.dma_start(out=cos_b[:], in_=cosv[:, 2:NT, :])
        load_x(3)
        load_words(1, 1)

        def flip(s):
            nc.gpsimd.tensor_scalar(out=s[:, :, 0:KD:2], in0=s[:, :, 0:KD:2], scalar1=-1.0, scalar2=0.0, op0=MULT, op1=ADD)

        def cos_of(i):
            return cos_a[:, i, :] if i < 2 else cos_b[:, i - 2, :]

        def sin_of(i):
            return sin_a[:, i, :] if i < 2 else sin_b[:, i - 2, :]

        perm = keep.tile([P, P], F32, name="perm")
        nc.gpsimd.tensor_copy(
            out=perm[:].rearrange("p (n e) -> p n e", e=2),
            in_=ident[:].rearrange("p (n e) -> p n e", e=2)[:, :, ::-1],
        )
        ident_bf = keep.tile([P, P], BF16, name="ident_bf")
        nc.gpsimd.tensor_copy(out=ident_bf[:], in_=ident[:])
        flip(sin_a)

        xc = keep.tile([P, 2, NG, 4, P], U32, name="xc", align_bytes=64)
        xsc = keep.tile([P, 2, NG, 4, P], U8, name="xsc", align_bytes=64)

        def turn(n, c):
            words = xg[n][:, c, :].bitcast(F32)
            xt = psum_t.tile([P, NG, 2, P], F32, name="xt")
            for g in range(NG):
                for u in range(2):
                    nc.tensor.transpose(xt[:, g, u, :], words[:, 256 * g + u : 256 * (g + 1) : 2], ident[:])
            nc.scalar.copy(out=grps[n][:, :, c].bitcast(F32), in_=xt[:].rearrange("p g u r -> p g r u"))

        def turn_pass(g):
            words = xg[0][:, 0, :].bitcast(F32)
            xt = psum_t.tile([P, 2, P], F32, name="xt")
            for u in range(2):
                nc.tensor.transpose(xt[:, u, :], words[:, 256 * g + u : 256 * (g + 1) : 2], ident[:])
            nc.scalar.copy(out=grps[0][:, g, 0].bitcast(F32), in_=xt[:].rearrange("p u r -> p r u"))

        coded = [0]

        def last_tile(unit):
            return unit[1] if unit[0] == "A" else 4 * unit[2] + 3

        def quantise(n):
            i0, cnt = X_GROUPS[n]
            coded[0] = i0 + cnt
            hf, il = divmod(i0, 4)
            if cnt == 4:
                nc.vector.quantize_mx(
                    out=xc[:, hf].rearrange("p g i w -> p (g i w)").bitcast(E5M2X4),
                    scales=xsc[:, hf].rearrange("p g i w -> p (g i w)"),
                    in_=grps[n][:].rearrange("p g c r t -> p (g c r t)"),
                )
            else:
                for g in range(NG):
                    nc.vector.quantize_mx(
                        out=xc[:, hf, g, il : il + cnt, :].rearrange("p i w -> p (i w)").bitcast(E5M2X4),
                        scales=xsc[:, hf, g, il : il + cnt, :].rearrange("p i w -> p (i w)"),
                        in_=grps[n][:, g].rearrange("p c r t -> p (c r t)"),
                    )

        cos_t = keep.tile([P, NT, P], BF16, name="cos_t")
        sin_t = keep.tile([P, NT, P], BF16, name="sin_t")
        sin_w = keep.tile([P, NT, KD], BF16, name="sin_w")

        def swap_sin():
            nc.scalar.mul(out=sin_b[:, :, 0:KD:2], in_=sin_b[:, :, 0:KD:2], mul=-1.0)
            for dst, src in ((sin_w[:, 0:2, :], sin_a), (sin_w[:, 2:NT, :], sin_b)):
                nc.scalar.copy(
                    out=dst.rearrange("p i (n e) -> p (i n) e", e=2),
                    in_=src[:].rearrange("p i (n e) -> p (i n) e", e=2)[:, :, ::-1],
                )

        def turn_table(dst, src_of):
            tt = psum_t.tile([P, NT, P], BF16, name="xt")
            for i in range(NT):
                nc.tensor.transpose(tt[:, i, :], src_of(i), ident_bf[:])
            nc.scalar.copy(out=dst[:], in_=tt[:])

        accs = {}
        pairs = {}
        stores = []
        step = [0]
        singles = {}
        prods = {}
        sums = {}

        def mx(unit):
            acc = psum_mx.tile([P, 512], F32, name="acc")
            accs[unit] = acc
            if unit[0] == "A":
                kind, i, m, jj = unit
                hf, il = divmod(i, 4)
                for g in range(NG):
                    nc.tensor.matmul_mx(
                        out=acc[:],
                        lhsT=xc[:, hf, g, il, :].bitcast(E5M2X4),
                        lhsT_scale=xsc[:, hf, g, il, :],
                        rhs=wt[(m, jj)][:, g, :].bitcast(E2M1X4),
                        rhs_scale=planes[m][:, g, 512 * jj : 512 * (jj + 1)],
                        start=(g == 0),
                        stop=(g == NG - 1),
                    )
            else:
                kind, hh, hf = unit
                for g in range(NG):
                    nc.tensor.matmul_mx(
                        out=acc[:],
                        lhsT=wt[(1, hh // 4)][:, g, 256 * (hh % 4) : 256 * (hh % 4 + 1)].bitcast(E2M1X4),
                        lhsT_scale=planes[1][:, g, P * hh : P * (hh + 1)],
                        rhs=xc[:, hf, g].rearrange("p i w -> p (i w)").bitcast(E5M2X4),
                        rhs_scale=xsc[:, hf, g].rearrange("p i w -> p (i w)"),
                        start=(g == 0),
                        stop=(g == NG - 1),
                    )

        def products_plain(unit, alone):
            kind, i, m, jj = unit
            acc = accs[unit]
            a, ii = divmod(i, 2)
            if alone:
                a1 = ab1_pool.tile([P, 4, 1, KD], F32, name="a1")
                b1 = ab1_pool.tile([P, 4, 1, KD], F32, name="b1")
                singles[unit] = (a1, b1)
                a2, b2, ii = a1, b1, 0
            else:
                if (a, m, jj) not in pairs:
                    a2 = ab_pool.tile([P, 4, 2, KD], F32, name="a2")
                    b2 = ab_pool.tile([P, 4, 2, KD], F32, name="b2")
                    pairs[(a, m, jj)] = (a2, b2)
                a2, b2 = pairs[(a, m, jj)]
            shape4 = [P, 4, KD // 2, 2]
            u_nat = acc[:].rearrange("p (h n e) -> p h n e", h=4, e=2)
            u_swp = u_nat[:, :, :, ::-1]
            cos4 = cos_of(i).rearrange("p (n e) -> p n e", e=2).unsqueeze(1).to_broadcast(shape4)
            sin4 = sin_of(i).rearrange("p (n e) -> p n e", e=2).unsqueeze(1).to_broadcast(shape4)
            a4 = a2[:, :, ii, :].rearrange("p h (n e) -> p h n e", e=2)
            b4 = b2[:, :, ii, :].rearrange("p h (n e) -> p h n e", e=2)
            if m == 0:
                nc.vector.tensor_tensor(out=a4, in0=u_nat, in1=cos4, op=MULT)
                nc.vector.tensor_tensor(out=b4, in0=u_swp, in1=sin4, op=MULT)
            else:
                nc.vector.scalar_tensor_tensor(out=a4, in0=u_nat, scalar=K_SCALE, in1=cos4, op0=MULT, op1=MULT)
                nc.vector.scalar_tensor_tensor(out=b4, in0=u_swp, scalar=K_SCALE, in1=sin4, op0=MULT, op1=MULT)

        def add_plain(unit):
            kind, i, m, jj = unit
            a = i // 2
            a2, b2 = pairs[(a, m, jj)]
            o = o_pool.tile([P, 4, 2, KD], F32, name="o")
            nc.gpsimd.tensor_tensor(
                out=o[:],
                in0=a2[:],
                in1=b2[:],
                op=ADD,
            )
            stores.append((step[0] + STORE_LAG, outs[m][:, 4 * jj : 4 * jj + 4, 2 * a : 2 * a + 2, :], o))

        def add_single(unit, engine):
            kind, i, m, jj = unit
            a1, b1 = singles[unit]
            o = o1_pool.tile([P, 4, KD], F32, name="o1")
            engine.tensor_tensor(out=o[:], in0=a1[:, :, 0, :], in1=b1[:, :, 0, :], op=ADD)
            stores.append((step[0] + (STORE_LAG if engine is nc.gpsimd else 0), outs[m][:, 4 * jj : 4 * jj + 4, i, :], o))

        def tables_of(hf):
            return (cos_t[:, 4 * hf : 4 * hf + 4, :].rearrange("p i r -> p (i r)"), sin_t[:, 4 * hf : 4 * hf + 4, :].rearrange("p i r -> p (i r)"))

        def products_turned(unit):
            kind, hh, hf = unit
            acc = accs[unit]
            if kind == "C":
                ac = cp_pool.tile([P, 512], F32, name="ac")
                bc = cp_pool.tile([P, 512], F32, name="bc")
                prods[unit] = (ac, bc)
                cos_s, sin_s = tables_of(hf)
                nc.vector.tensor_tensor(out=ac[:], in0=acc[:], in1=cos_s, op=MULT)
                nc.vector.tensor_tensor(out=bc[:], in0=acc[:], in1=sin_s, op=MULT)
            else:
                u = u_pool.tile([P, 512], F32, name="u")
                prods[unit] = u
                nc.scalar.copy(out=u[:], in_=acc[:])

        def products_pool(unit):
            kind, hh, hf = unit
            u = prods[unit]
            ac = cp_pool.tile([P, 512], F32, name="ag")
            bc = cp_pool.tile([P, 512], F32, name="bg")
            prods[unit] = (ac, bc)
            cos_s, sin_s = tables_of(hf)
            nc.gpsimd.tensor_tensor(out=ac[:], in0=u[:], in1=cos_s, op=MULT)
            nc.gpsimd.tensor_tensor(out=bc[:], in0=u[:], in1=sin_s, op=MULT)

        def sum_turned(unit):
            ac, bc = prods[unit]
            ct = psum_t.tile([P, 4, KD], F32, name="xt")
            sums[unit] = ct
            for blk in range(4):
                cols = slice(P * blk, P * (blk + 1))
                nc.tensor.matmul(out=ct[:, blk, :], lhsT=ac[:, cols], rhs=ident[:], is_transpose=True, start=True, stop=False)
                nc.tensor.matmul(out=ct[:, blk, :], lhsT=bc[:, cols], rhs=perm[:], is_transpose=True, start=False, stop=True)

        def store_turned(unit):
            kind, hh, hf = unit
            oc = oc_pool.tile([P, 4, KD], F32, name="oc")
            nc.scalar.mul(out=oc[:], in_=sums[unit][:], mul=K_SCALE)
            nc.sync.dma_start(out=outs[1][:, hh, 4 * hf : 4 * hf + 4, :], in_=oc[:])

        def plain_units(a):
            return [("A", 2 * a + ii, m, jj) for m, jj in PLAIN for ii in range(2)]

        seq = [("A", 0, 0, 0), ("A", 0, 0, 1), ("A", 1, 0, 0), ("A", 1, 0, 1), ("A", 0, 1, 0), ("A", 1, 1, 0)]
        seq += plain_units(1)
        pair_list = [[("A", 2 * a + ii, m, jj) for ii in range(2)] for a in (2, 3) for m, jj in PLAIN[:2]]
        turned_list = [(hh, 0) for hh in range(4, 8)] + [(hh, 1) for hh in range(8)]
        for tok in ORDER:
            if tok == "p":
                seq += pair_list[0]
                pair_list = pair_list[1:]
            else:
                seq.append(({"c": "C", "b": "B"}[tok],) + turned_list[0])
                turned_list = turned_list[1:]

        extra = {1: [(quantise, 1)], 5: [(quantise, 2)], Q3_AT: [(quantise, 3)]}
        later = {1: [(turn, 2, 0), (turn, 2, 1)],
                 3: [(turn_table, cos_t, cos_of), (swap_sin,)],
                 5: [(turn, 3, 0), (turn, 3, 1)],
                 6: [(turn, 3, 2), (turn, 3, 3)],
                 8: [(turn_table, sin_t, lambda i: sin_w[:, i, :])]}

        turn_pass(0)
        turn_pass(1)
        spin(SPIN_GAP)
        quantise(0)
        mx(seq[0])
        turn(1, 0)
        mx(seq[1])
        n_seq = len(seq)
        issued = 2
        seen = []
        for idx in range(n_seq + B_LAG + 2):
            step[0] = idx
            for job in extra.get(idx, ()):
                job[0](*job[1:])
            while issued < min(n_seq, idx + LOOK + 1) and last_tile(seq[issued]) < coded[0]:
                mx(seq[issued])
                issued += 1
            for job in later.get(idx, ()):
                job[0](*job[1:])
            if 1 <= idx <= n_seq and seq[idx - 1][0] == "C":
                sum_turned(seq[idx - 1])
            if B_LAG <= idx < n_seq + B_LAG and seq[idx - B_LAG][0] == "B":
                sum_turned(seq[idx - B_LAG])
            if idx < n_seq:
                unit = seq[idx]
                if unit[0] == "A":
                    mode = ADD_MODE.get(idx, "p")
                    products_plain(unit, mode != "p")
                    if mode == "g":
                        add_single(unit, nc.gpsimd)
                    elif mode == "v":
                        add_single(unit, nc.vector)
                    elif ("A", unit[1] ^ 1, unit[2], unit[3]) in seen:
                        add_plain(unit)
                    seen.append(unit)
                else:
                    products_turned(unit)
                    if unit[0] == "B":
                        products_pool(unit)
            for due, view, tile_ in list(stores):
                if due <= idx:
                    nc.sync.dma_start(out=view, in_=tile_[:])
                    stores.remove((due, view, tile_))
            if 2 <= idx <= n_seq + 1 and seq[idx - 2][0] == "C":
                store_turned(seq[idx - 2])
            if B_LAG + 1 <= idx < n_seq + B_LAG + 1 and seq[idx - B_LAG - 1][0] == "B":
                store_turned(seq[idx - B_LAG - 1])
